import numpy as np
import ml_dtypes


def mxq(x, axis, fmt="e4m3"):
    dtype, down = {"e4m3": (ml_dtypes.float8_e4m3fn, 7), "e5m2": (ml_dtypes.float8_e5m2, 14)}[fmt]
    v = np.moveaxis(np.asarray(x, np.float32).astype(ml_dtypes.bfloat16).astype(np.float64), axis, -1)
    blocks = v.reshape(v.shape[:-1] + (-1, 32))
    amax = np.abs(blocks).max(-1, keepdims=True)
    byte = np.maximum(np.where(amax > 0, np.frexp(amax)[1] - 1 + 127, 0) - down, 1)
    scale = np.exp2(byte - 127.0)
    codes = (blocks / scale).astype(np.float32).astype(dtype).astype(np.float64)
    return np.moveaxis((codes * scale).reshape(v.shape), -1, axis)


WIDE = False


def mx_kscale(k):
    if not WIDE:
        return np.ones(k)
    levels = np.array([10, -10, 5, -5, 0])
    a = np.random.permutation(np.resize(levels, k // 512 * 4)).reshape(k // 512, 4)
    idx = np.arange(k)
    return np.exp2(a[idx // 512, idx % 128 // 32])


BF16 = ml_dtypes.bfloat16


def bf(x):
    return np.asarray(x, np.float32).astype(BF16)


def f64(x):
    return np.asarray(x).astype(np.float64)


E2M1 = np.array([0.0, 0.5, 1.0, 1.5, 2.0, 3.0, 4.0, 6.0, -0.0, -0.5, -1.0, -1.5, -2.0, -3.0, -4.0, -6.0])


def pack_weight(w, fmt):
    k, n = w.shape
    w = f64(bf(w)).reshape(k // 32, 32, n)
    amax = np.abs(w).max(1)
    if fmt == "e4m3":
        byte = np.frexp(amax)[1] - 1 + 127 - 7
    else:
        mant, ex = np.frexp(amax / 6.0)
        byte = np.where(mant > 0.5, ex, ex - 1) + 127
    byte = np.clip(np.where(amax > 0, byte, 1), 1, 254)
    scaled = (w * np.exp2(127.0 - byte)[:, None, :]).reshape(k, n).astype(np.float32)
    by_word = np.ascontiguousarray(scaled.reshape(k // 512, 128, 4, n).transpose(0, 1, 3, 2))
    if fmt == "e4m3":
        words = by_word.astype(ml_dtypes.float8_e4m3fn).view(np.uint8)
    else:
        c = by_word.astype(ml_dtypes.float4_e2m1fn).view(np.uint8) & 0xF
        words = c[..., 0::2] | (c[..., 1::2] << 4)
    return np.ascontiguousarray(words), np.ascontiguousarray(byte.astype(np.uint8).reshape(k // 512, 16, n))


def unpack_weight(words, scales, fmt):
    g, p, n, _ = words.shape
    if fmt == "e4m3":
        vals = np.ascontiguousarray(words).view(ml_dtypes.float8_e4m3fn).astype(np.float64)
    else:
        nib = np.empty((g, p, n, 4), np.uint8)
        nib[..., 0::2] = words & 0xF
        nib[..., 1::2] = words >> 4
        vals = E2M1[nib]
    vals = vals * np.repeat(np.exp2(scales.astype(np.float64) - 127.0), 8, axis=1)[..., None]
    return vals.transpose(0, 1, 3, 2).reshape(g * 512, n)


B, STOCH, ACT_DIM, HIDDEN, DETER = 128, 256, 256, 16384, 1024
K1 = STOCH + ACT_DIM
EPS = 1e-4
FMT = "e4m3"


def silu(v):
    return v / (1.0 + np.exp(-v))


def rmsnorm(v, w):
    return v * (1.0 / np.sqrt(np.mean(v * v, axis=-1, keepdims=True) + EPS)) * w


def setup_inputs():
    s = mx_kscale(K1)[:STOCH]
    w1 = np.random.standard_normal((HIDDEN, K1)) * 0.07 / np.sqrt(K1)
    w1[:, :STOCH] = w1[:, :STOCH] / s
    stoch = bf(np.random.standard_normal((B, STOCH)) * s)
    action = bf(np.random.standard_normal((B, ACT_DIM)))
    w1_words, w1_scales = pack_weight(np.ascontiguousarray(w1.T), FMT)
    tok_b1 = bf(np.random.standard_normal(HIDDEN) * 0.03)
    tok_nw = bf(1.0 + 0.1 * np.random.standard_normal(HIDDEN))
    w2 = np.random.standard_normal((DETER, HIDDEN)) * 1.5 / np.sqrt(HIDDEN)
    w2_words, w2_scales = pack_weight(np.ascontiguousarray(w2.T), FMT)
    tok_b2 = bf(np.random.standard_normal(DETER) * 0.2)
    return {"stoch": stoch,
            "action": action,
            "tok_w1_words": w1_words,
            "tok_w1_scales": w1_scales,
            "tok_b1": tok_b1,
            "tok_nw": tok_nw,
            "tok_w2_words": w2_words,
            "tok_w2_scales": w2_scales,
            "tok_b2": tok_b2}


def reference(stoch, action, tok_w1_words, tok_w1_scales, tok_b1, tok_nw, tok_w2_words, tok_w2_scales, tok_b2):
    act = f64(action)
    act = act / np.maximum(np.abs(act), 1.0)
    u = np.concatenate([f64(stoch), act], axis=-1)
    h = (mxq(u, 1, "e4m3") @ unpack_weight(tok_w1_words, tok_w1_scales, FMT)) + f64(tok_b1)
    g = silu(rmsnorm(h, f64(tok_nw)))
    return (mxq(g, 1, "e4m3") @ unpack_weight(tok_w2_words, tok_w2_scales, FMT)) + f64(tok_b2)

@@ -1,0 +1,259 @@
+from contextlib import ExitStack
+
+import concourse.mybir as mybir
+from concourse.masks import make_identity
+
+F32 = mybir.dt.float32
+BF16 = mybir.dt.bfloat16
+I32 = mybir.dt.int32
+U32 = mybir.dt.uint32
+U8 = mybir.dt.uint8
+FP8X4 = mybir.dt.float8_e4m3fn_x4
+ALU = mybir.AluOpType
+FUNC = mybir.ActivationFunctionType
+
+P = 128
+PACK = 4
+K_PASS = P * PACK
+N_PASS = 512
+STOCH = 256
+HIDDEN = 16384
+DETER = 1024
+EPS = 1e-4
+
+CHUNK = 2048
+UNIT = 1024
+UNITS = HIDDEN // UNIT
+W1_CHUNKS = HIDDEN // CHUNK
+ROW = 256
+PLANES = 4
+B1_LEAD = 3
+
+FLOPS = 2 * P * K_PASS * HIDDEN + 2 * P * HIDDEN * DETER
+
+
+def tile_mamba2backbone_pa_k_kernel(
+    tc, stoch, action, tok_w1_words, tok_w1_scales, tok_b1, tok_nw, tok_w2_words, tok_w2_scales, tok_b2, out
+):
+    nc = tc.nc
+    with ExitStack() as stack:
+        keep = stack.enter_context(tc.tile_pool(name="keep", bufs=1))
+        weights = stack.enter_context(tc.tile_pool(name="weights", bufs=10))
+        b1_pool = stack.enter_context(tc.tile_pool(name="b1_pool", bufs=B1_LEAD + 1))
+        work = stack.enter_context(tc.tile_pool(name="work", bufs=4))
+        psum_mm = stack.enter_context(tc.psum_pool(name="psum_mm", bufs=4))
+        psum_bc = stack.enter_context(tc.psum_pool(name="psum_bc", bufs=2))
+        psum_acc = stack.enter_context(tc.psum_pool(name="psum_acc", bufs=1))
+
+        u_sb = keep.tile([P, K_PASS], BF16)
+        act_sb = keep.tile([P, K_PASS - STOCH], BF16)
+        nc.scalar.dma_start(out=u_sb[:, 0:STOCH], in_=stoch)
+        nc.scalar.dma_start(out=act_sb[:], in_=action)
+
+        table = keep.tile([P, 2 * P], F32)
+        nc.vector.memset(table[:, P : 2 * P], 0.0)
+        nc.scalar.dma_start(out=table[0:64, 0:P], in_=tok_b1.bitcast(F32).rearrange("(r w) -> r w", w=P))
+        nc.scalar.dma_start(out=table[64:P, 0:P], in_=tok_nw.bitcast(F32).rearrange("(r w) -> r w", w=P))
+        nc.scalar.dma_start(out=table[0:4, P : 2 * P], in_=tok_b2.bitcast(F32).rearrange("(r w) -> r w", w=P))
+        B1_ROW0, NW_ROW0, B2_ROW0 = 0, 64, P
+
+        ident = keep.tile([P, P], F32)
+        make_identity(nc, ident[:])
+
+        warm = keep.tile([P, 1], F32)
+        nc.vector.memset(warm[:], 0.0)
+        nc.scalar.activation(out=warm[:], in_=warm[:], func=FUNC.Silu)
+
+        neg_half = keep.tile([P, 1], F32)
+        nc.vector.memset(neg_half[:], -0.5)
+
+        w1_planes = keep.tile([P, HIDDEN // PLANES], U8, align_bytes=64)
+        w2_planes = keep.tile([P, HIDDEN // K_PASS // PLANES, DETER], U8, align_bytes=64)
+        nc.vector.memset(w1_planes[:].bitcast(I32), 0)
+        nc.vector.memset(w2_planes[:].rearrange("p a n -> p (a n)").bitcast(I32), 0)
+
+        for quad in range(4):
+            nc.sync.dma_start(
+                out=w1_planes[32 * quad : 32 * quad + 16, :].bitcast(I32),
+                in_=tok_w1_scales[0, 4 * quad : 4 * quad + 4, :].bitcast(I32).rearrange("r (k c) -> k r c", k=PLANES),
+            )
+
+        def load_w2_planes(a):
+            for quad in range(4):
+                nc.sync.dma_start(
+                    out=w2_planes[32 * quad : 32 * quad + 16, a, :].bitcast(I32),
+                    in_=tok_w2_scales[PLANES * a : PLANES * (a + 1), 4 * quad : 4 * quad + 4, :].bitcast(I32),
+                )
+
+        w1_words = tok_w1_words[0].rearrange("p n t -> p (n t)").bitcast(I32)
+        w2_words = tok_w2_words.rearrange("g p n t -> p g (n t)").bitcast(I32)
+        w1_tiles = []
+        for c in range(W1_CHUNKS):
+            w1_tile = weights.tile([P, CHUNK], U32, tag="w", name="w1_tile", align_bytes=64)
+            nc.sync.dma_start(out=w1_tile[:].bitcast(I32), in_=w1_words[:, c * CHUNK : (c + 1) * CHUNK])
+            w1_tiles.append(w1_tile)
+        w2_tiles = []
+        for i in range(UNITS):
+            if i % 8 == 0:
+                for a in range(i // 2, i // 2 + 4):
+                    load_w2_planes(a)
+            w2_tile = weights.tile([P, CHUNK], U32, tag="w", name="w2_tile", align_bytes=64)
+            nc.sync.dma_start(
+                out=w2_tile[:].bitcast(I32).rearrange("p (g n) -> p g n", g=2), in_=w2_words[:, 2 * i : 2 * i + 2, :]
+            )
+            w2_tiles.append(w2_tile)
+
+        turned_ps = psum_bc.tile([P, N_PASS], F32, tag="bc", name="turned_ps")
+        for half in range(2):
+            nc.tensor.transpose(turned_ps[:, half * P : (half + 1) * P], table[:, half * P : (half + 1) * P], ident[:])
+        turned = keep.tile([P, 2 * P], F32)
+        nc.vector.tensor_copy(out=turned[:], in_=turned_ps[:, 0 : 2 * P])
+
+        def spread(first_row):
+            bank = psum_bc.tile([P, N_PASS], F32, tag="bc", name="bank")
+            for r in range(4):
+                nc.tensor.transpose(
+                    bank[:, r * P : (r + 1) * P],
+                    turned[:, first_row + r : first_row + r + 1].to_broadcast([P, P]),
+                    ident[:],
+                )
+            return bank
+
+        nc.vector.tensor_scalar(
+            out=u_sb[:, STOCH:K_PASS], in0=act_sb[:], scalar1=-1.0, scalar2=1.0, op0=ALU.max, op1=ALU.min
+        )
+        u_words = u_sb[:].bitcast(F32)
+        u_ps = psum_mm.tile([P, 2, P], F32, tag="mm", name="u_ps")
+        for w in range(2):
+            nc.tensor.transpose(u_ps[:, w, :], u_words[:, w : K_PASS // 2 : 2], ident[:])
+        u_grouped = keep.tile([P, P * PACK], BF16, align_bytes=64)
+        nc.vector.tensor_copy(
+            out=u_grouped[:].bitcast(F32).rearrange("p (b w) -> p b w", w=2), in_=u_ps[:].rearrange("p w b -> p b w")
+        )
+        u_codes = keep.tile([P, P], U32, align_bytes=64)
+        u_plane = keep.tile([P, P], U8, align_bytes=64)
+        nc.vector.quantize_mx(out=u_codes[:].bitcast(FP8X4), scales=u_plane[:], in_=u_grouped[:])
+
+        b2_bank = spread(B2_ROW0)
+        b2_all = keep.tile([P, DETER], BF16)
+        nc.scalar.copy(out=b2_all[:].bitcast(F32), in_=b2_bank[:])
+
+        h = [keep.tile([P, UNIT], F32, name="h%d" % i) for i in range(UNITS)]
+        sums = keep.tile([P, UNITS], F32)
+        b1_tiles = {}
+
+        def spread_b1(c):
+            b1_all = b1_pool.tile([P, CHUNK], BF16, name="b1_all")
+            for half in range(2):
+                bank = spread(B1_ROW0 + (CHUNK // ROW) * c + 4 * half)
+                dst = b1_all[:].bitcast(F32)[:, half * N_PASS : (half + 1) * N_PASS]
+                if half == 0:
+                    nc.scalar.copy(out=dst, in_=bank[:])
+                else:
+                    nc.vector.tensor_copy(out=dst, in_=bank[:])
+            b1_tiles[c] = b1_all
+
+        def first_layer(c):
+            for j in range(CHUNK // N_PASS):
+                n = c * (CHUNK // N_PASS) + j
+                k, col = divmod(n * N_PASS, HIDDEN // PLANES)
+                h_ps = psum_mm.tile([P, N_PASS], F32, tag="mm", name="h_ps")
+                nc.tensor.matmul_mx(
+                    out=h_ps[:],
+                    lhsT=u_codes[:].bitcast(FP8X4),
+                    lhsT_scale=u_plane[:],
+                    rhs=w1_tiles[c][:, j * N_PASS : (j + 1) * N_PASS].bitcast(FP8X4),
+                    rhs_scale=w1_planes[4 * k : P, col : col + N_PASS],
+                    start=True,
+                    stop=True,
+                )
+                nc.vector.tensor_tensor(
+                    out=h[n // 2][:, (n % 2) * N_PASS : (n % 2 + 1) * N_PASS],
+                    in0=h_ps[:],
+                    in1=b1_tiles[c][:, j * N_PASS : (j + 1) * N_PASS],
+                    op=ALU.add,
+                )
+            for i in range(c * (CHUNK // UNIT), (c + 1) * (CHUNK // UNIT)):
+                squares = work.tile([P, UNIT], BF16, name="squares")
+                nc.scalar.activation(out=squares[:], in_=h[i][:], func=FUNC.Square, accum_out=sums[:, i : i + 1])
+
+        for c in range(B1_LEAD):
+            spread_b1(c)
+        for c in range(W1_CHUNKS):
+            if c + B1_LEAD < W1_CHUNKS:
+                spread_b1(c + B1_LEAD)
+            first_layer(c)
+
+        total = keep.tile([P, 1], F32)
+        nc.vector.reduce_sum(out=total[:], in_=sums[:], axis=mybir.AxisListType.X)
+        mean_eps = keep.tile([P, 1], F32)
+        nc.vector.tensor_scalar(
+            out=mean_eps[:], in0=total[:], scalar1=1.0 / HIDDEN, scalar2=EPS, op0=ALU.mult, op1=ALU.add
+        )
+        rstd = keep.tile([P, 1], F32)
+        nc.gpsimd.tensor_tensor(out=rstd[:], in0=mean_eps[:], in1=neg_half[:], op=ALU.pow)
+
+        acc = [psum_acc.tile([P, N_PASS], F32, name="acc%d" % half) for half in range(2)]
+        v_tiles = {}
+        g_tiles = {}
+
+        def normalise(i):
+            nw_bank = spread(NW_ROW0 + (UNIT // ROW) * i)
+            nw_all = nw_bank[:].bitcast(BF16)
+            v_tiles[i] = []
+            for s in range(UNIT // K_PASS):
+                v = work.tile([P, PACK, P], F32, name="v")
+                cols = slice(s * K_PASS, (s + 1) * K_PASS)
+                nc.vector.scalar_tensor_tensor(
+                    out=v[:],
+                    in0=h[i][:, cols].rearrange("b (q t) -> b t q", t=PACK),
+                    scalar=rstd[:, 0:1],
+                    in1=nw_all[:, cols].rearrange("b (q t) -> b t q", t=PACK),
+                    op0=ALU.mult,
+                    op1=ALU.mult,
+                )
+                v_tiles[i].append(v)
+
+        def turn_and_quantise(i):
+            grouped = work.tile([P, UNIT // K_PASS, P, PACK], BF16, name="grouped", align_bytes=64)
+            for s in range(UNIT // K_PASS):
+                v_ps = psum_mm.tile([P, PACK, P], F32, tag="mm", name="v_ps")
+                for t in range(PACK):
+                    nc.tensor.transpose(v_ps[:, t, :], v_tiles[i][s][:, t, :], ident[:])
+                nc.scalar.activation(out=grouped[:, s, :, :], in_=v_ps[:].rearrange("p t b -> p b t"), func=FUNC.Silu)
+            g_codes = work.tile([P, UNIT // PACK], U32, name="g_codes", align_bytes=64)
+            g_plane = work.tile([P, UNIT // PACK], U8, name="g_plane", align_bytes=64)
+            nc.vector.quantize_mx(
+                out=g_codes[:].bitcast(FP8X4), scales=g_plane[:], in_=grouped[:].rearrange("p s b t -> p (s b t)")
+            )
+            g_tiles[i] = (g_codes, g_plane)
+
+        def second_layer(i):
+            g_codes, g_plane = g_tiles[i]
+            for s in range(UNIT // K_PASS):
+                g_pass = i * (UNIT // K_PASS) + s
+                a, k = divmod(g_pass, PLANES)
+                for half in range(2):
+                    nc.tensor.matmul_mx(
+                        out=acc[half][:],
+                        lhsT=g_codes[:, s * P : (s + 1) * P].bitcast(FP8X4),
+                        lhsT_scale=g_plane[:, s * P : (s + 1) * P],
+                        rhs=w2_tiles[i][:, s * DETER + half * N_PASS : s * DETER + (half + 1) * N_PASS].bitcast(FP8X4),
+                        rhs_scale=w2_planes[4 * k : P, a, half * N_PASS : (half + 1) * N_PASS],
+                        start=(g_pass == 0),
+                        stop=(g_pass == HIDDEN // K_PASS - 1),
+                    )
+
+        for i in range(UNITS + 2):
+            if i < UNITS:
+                normalise(i)
+            if 1 <= i <= UNITS:
+                turn_and_quantise(i - 1)
+            if i >= 2:
+                second_layer(i - 2)
+
+        out_sb = keep.tile([P, DETER], F32)
+        for half in range(2):
+            cols = slice(half * N_PASS, (half + 1) * N_PASS)
+            nc.vector.tensor_tensor(out=out_sb[:, cols], in0=acc[half][:], in1=b2_all[:, cols], op=ALU.add)
+            nc.sync.dma_start(out=out[:, cols], in_=out_sb[:, cols])

@@ -37,6 +37,7 @@ def tile_mamba2backbone_pa_k_kernel(
 ):
     nc = tc.nc
     with ExitStack() as stack:
+        stack.enter_context(tc.manual_schedule())
         keep = stack.enter_context(tc.tile_pool(name="keep", bufs=1))
         weights = stack.enter_context(tc.tile_pool(name="weights", bufs=10))
         b1_pool = stack.enter_context(tc.tile_pool(name="b1_pool", bufs=B1_LEAD + 1))
@@ -205,10 +206,10 @@ def tile_mamba2backbone_pa_k_kernel(
                 v = work.tile([P, PACK, P], F32, name="v")
                 cols = slice(s * K_PASS, (s + 1) * K_PASS)
                 nc.vector.scalar_tensor_tensor(
-                    out=v[:],
-                    in0=h[i][:, cols].rearrange("b (q t) -> b t q", t=PACK),
+                    out=v[:].rearrange("b t q -> b q t"),
+                    in0=h[i][:, cols].rearrange("b (q t) -> b q t", t=PACK),
                     scalar=rstd[:, 0:1],
-                    in1=nw_all[:, cols].rearrange("b (q t) -> b t q", t=PACK),
+                    in1=nw_all[:, cols].rearrange("b (q t) -> b q t", t=PACK),
                     op0=ALU.mult,
                     op1=ALU.mult,
                 )

@@ -28,6 +28,7 @@ W1_CHUNKS = HIDDEN // CHUNK
 ROW = 256
 PLANES = 4
 B1_LEAD = 3
+GAIN_LEAD = 2
 
 FLOPS = 2 * P * K_PASS * HIDDEN + 2 * P * HIDDEN * DETER
 
@@ -185,6 +186,13 @@ def tile_mamba2backbone_pa_k_kernel(
                 spread_b1(c + B1_LEAD)
             first_layer(c)
 
+        def scale_by_gain(i):
+            nw_bank = spread(NW_ROW0 + (UNIT // ROW) * i)
+            nc.vector.tensor_tensor(out=h[i][:], in0=h[i][:], in1=nw_bank[:].bitcast(BF16), op=ALU.mult)
+
+        for i in range(GAIN_LEAD):
+            scale_by_gain(i)
+
         total = keep.tile([P, 1], F32)
         nc.vector.reduce_sum(out=total[:], in_=sums[:], axis=mybir.AxisListType.X)
         mean_eps = keep.tile([P, 1], F32)
@@ -195,44 +203,48 @@ def tile_mamba2backbone_pa_k_kernel(
         nc.gpsimd.tensor_tensor(out=rstd[:], in0=mean_eps[:], in1=neg_half[:], op=ALU.pow)
 
         acc = [psum_acc.tile([P, N_PASS], F32, name="acc%d" % half) for half in range(2)]
-        v_tiles = {}
+        g_rows_tiles = {}
+        g_ps_tiles = {}
         g_tiles = {}
+        PASSES = UNIT // K_PASS
 
-        def normalise(i):
-            nw_bank = spread(NW_ROW0 + (UNIT // ROW) * i)
-            nw_all = nw_bank[:].bitcast(BF16)
-            v_tiles[i] = []
-            for s in range(UNIT // K_PASS):
-                v = work.tile([P, PACK, P], F32, name="v")
-                cols = slice(s * K_PASS, (s + 1) * K_PASS)
-                nc.vector.scalar_tensor_tensor(
-                    out=v[:].rearrange("b t q -> b q t"),
-                    in0=h[i][:, cols].rearrange("b (q t) -> b q t", t=PACK),
-                    scalar=rstd[:, 0:1],
-                    in1=nw_all[:, cols].rearrange("b (q t) -> b q t", t=PACK),
-                    op0=ALU.mult,
-                    op1=ALU.mult,
-                )
-                v_tiles[i].append(v)
+        def activate(i):
+            g_rows = work.tile([P, UNIT], BF16, name="g_rows")
+            nc.scalar.activation(
+                out=g_rows[:].rearrange("b (w q e) -> b w q e", w=2, e=2),
+                in_=h[i][:].rearrange("b (q w e) -> b w q e", w=2, e=2),
+                func=FUNC.Silu,
+                scale=rstd[:, 0:1],
+            )
+            g_rows_tiles[i] = g_rows
 
-        def turn_and_quantise(i):
-            grouped = work.tile([P, UNIT // K_PASS, P, PACK], BF16, name="grouped", align_bytes=64)
-            for s in range(UNIT // K_PASS):
-                v_ps = psum_mm.tile([P, PACK, P], F32, tag="mm", name="v_ps")
-                for t in range(PACK):
-                    nc.tensor.transpose(v_ps[:, t, :], v_tiles[i][s][:, t, :], ident[:])
-                nc.scalar.activation(out=grouped[:, s, :, :], in_=v_ps[:].rearrange("p t b -> p b t"), func=FUNC.Silu)
+        def turn(i):
+            g_words = g_rows_tiles[i][:].bitcast(F32)
+            g_ps = psum_mm.tile([P, PASSES, 2, P], F32, tag="mm", name="g_ps")
+            for s in range(PASSES):
+                for w in range(2):
+                    first = w * (UNIT // PACK) + s * P
+                    nc.tensor.transpose(g_ps[:, s, w, :], g_words[:, first : first + P], ident[:])
+            g_ps_tiles[i] = g_ps
+
+        def group(i):
+            grouped = work.tile([P, UNIT], BF16, name="grouped", align_bytes=64)
+            nc.scalar.copy(
+                out=grouped[:].bitcast(F32).rearrange("p (s b w) -> p s b w", s=PASSES, w=2),
+                in_=g_ps_tiles[i][:].rearrange("p s w b -> p s b w"),
+            )
+            g_tiles[i] = grouped
+
+        def quantise(i):
             g_codes = work.tile([P, UNIT // PACK], U32, name="g_codes", align_bytes=64)
             g_plane = work.tile([P, UNIT // PACK], U8, name="g_plane", align_bytes=64)
-            nc.vector.quantize_mx(
-                out=g_codes[:].bitcast(FP8X4), scales=g_plane[:], in_=grouped[:].rearrange("p s b t -> p (s b t)")
-            )
+            nc.vector.quantize_mx(out=g_codes[:].bitcast(FP8X4), scales=g_plane[:], in_=g_tiles[i][:])
             g_tiles[i] = (g_codes, g_plane)
 
         def second_layer(i):
             g_codes, g_plane = g_tiles[i]
-            for s in range(UNIT // K_PASS):
-                g_pass = i * (UNIT // K_PASS) + s
+            for s in range(PASSES):
+                g_pass = i * PASSES + s
                 a, k = divmod(g_pass, PLANES)
                 for half in range(2):
                     nc.tensor.matmul_mx(
@@ -245,13 +257,18 @@ def tile_mamba2backbone_pa_k_kernel(
                         stop=(g_pass == HIDDEN // K_PASS - 1),
                     )
 
-        for i in range(UNITS + 2):
-            if i < UNITS:
-                normalise(i)
-            if 1 <= i <= UNITS:
-                turn_and_quantise(i - 1)
-            if i >= 2:
-                second_layer(i - 2)
+        for j in range(UNITS + 3):
+            if j + GAIN_LEAD < UNITS:
+                scale_by_gain(j + GAIN_LEAD)
+            if j < UNITS:
+                activate(j)
+            if 1 <= j <= UNITS:
+                turn(j - 1)
+                group(j - 1)
+            if 2 <= j <= UNITS + 1:
+                quantise(j - 2)
+            if j >= 3:
+                second_layer(j - 3)
 
         out_sb = keep.tile([P, DETER], F32)
         for half in range(2):

@@ -27,7 +27,7 @@ UNITS = HIDDEN // UNIT
 W1_CHUNKS = HIDDEN // CHUNK
 ROW = 256
 PLANES = 4
-B1_LEAD = 3
+WARM = 6
 GAIN_LEAD = 2
 
 FLOPS = 2 * P * K_PASS * HIDDEN + 2 * P * HIDDEN * DETER
@@ -41,11 +41,17 @@ def tile_mamba2backbone_pa_k_kernel(
         stack.enter_context(tc.manual_schedule())
         keep = stack.enter_context(tc.tile_pool(name="keep", bufs=1))
         weights = stack.enter_context(tc.tile_pool(name="weights", bufs=10))
-        b1_pool = stack.enter_context(tc.tile_pool(name="b1_pool", bufs=B1_LEAD + 1))
         work = stack.enter_context(tc.tile_pool(name="work", bufs=4))
-        psum_mm = stack.enter_context(tc.psum_pool(name="psum_mm", bufs=4))
-        psum_bc = stack.enter_context(tc.psum_pool(name="psum_bc", bufs=2))
+        junk = stack.enter_context(tc.tile_pool(name="junk", bufs=2))
+        psum = stack.enter_context(tc.psum_pool(name="psum", bufs=6))
         psum_acc = stack.enter_context(tc.psum_pool(name="psum_acc", bufs=1))
+
+        zero_words = keep.tile([P, N_PASS // 2], F32)
+        nc.vector.memset(zero_words[:], 0.0)
+        zeros = zero_words[:].bitcast(BF16)
+        for n in range(WARM):
+            idle_ps = psum.tile([P, N_PASS], F32, tag="bank", name="idle_ps")
+            nc.tensor.matmul(idle_ps[:], lhsT=zeros[:, 0:P], rhs=zeros, start=True, stop=True)
 
         u_sb = keep.tile([P, K_PASS], BF16)
         act_sb = keep.tile([P, K_PASS - STOCH], BF16)
@@ -105,14 +111,14 @@ def tile_mamba2backbone_pa_k_kernel(
             )
             w2_tiles.append(w2_tile)
 
-        turned_ps = psum_bc.tile([P, N_PASS], F32, tag="bc", name="turned_ps")
+        turned_ps = psum.tile([P, N_PASS], F32, tag="bank", name="turned_ps")
         for half in range(2):
             nc.tensor.transpose(turned_ps[:, half * P : (half + 1) * P], table[:, half * P : (half + 1) * P], ident[:])
         turned = keep.tile([P, 2 * P], F32)
         nc.vector.tensor_copy(out=turned[:], in_=turned_ps[:, 0 : 2 * P])
 
         def spread(first_row):
-            bank = psum_bc.tile([P, N_PASS], F32, tag="bc", name="bank")
+            bank = psum.tile([P, N_PASS], F32, tag="bank", name="bank")
             for r in range(4):
                 nc.tensor.transpose(
                     bank[:, r * P : (r + 1) * P],
@@ -125,7 +131,7 @@ def tile_mamba2backbone_pa_k_kernel(
             out=u_sb[:, STOCH:K_PASS], in0=act_sb[:], scalar1=-1.0, scalar2=1.0, op0=ALU.max, op1=ALU.min
         )
         u_words = u_sb[:].bitcast(F32)
-        u_ps = psum_mm.tile([P, 2, P], F32, tag="mm", name="u_ps")
+        u_ps = psum.tile([P, 2, P], F32, tag="bank", name="u_ps")
         for w in range(2):
             nc.tensor.transpose(u_ps[:, w, :], u_words[:, w : K_PASS // 2 : 2], ident[:])
         u_grouped = keep.tile([P, P * PACK], BF16, align_bytes=64)
@@ -136,30 +142,26 @@ def tile_mamba2backbone_pa_k_kernel(
         u_plane = keep.tile([P, P], U8, align_bytes=64)
         nc.vector.quantize_mx(out=u_codes[:].bitcast(FP8X4), scales=u_plane[:], in_=u_grouped[:])
 
+        h = [keep.tile([P, UNIT], F32, name="h%d" % i) for i in range(UNITS)]
+        sums = keep.tile([P, UNITS + 2], F32)
+
+        b1_all = keep.tile([P, HIDDEN], BF16)
+        for i in range(UNITS):
+            bank = spread(B1_ROW0 + (UNIT // ROW) * i)
+            dst = b1_all[:, i * UNIT : (i + 1) * UNIT].bitcast(F32)
+            if i % 2 == 0:
+                nc.scalar.copy(out=dst, in_=bank[:])
+            else:
+                nc.vector.tensor_copy(out=dst, in_=bank[:])
         b2_bank = spread(B2_ROW0)
         b2_all = keep.tile([P, DETER], BF16)
         nc.scalar.copy(out=b2_all[:].bitcast(F32), in_=b2_bank[:])
-
-        h = [keep.tile([P, UNIT], F32, name="h%d" % i) for i in range(UNITS)]
-        sums = keep.tile([P, UNITS], F32)
-        b1_tiles = {}
-
-        def spread_b1(c):
-            b1_all = b1_pool.tile([P, CHUNK], BF16, name="b1_all")
-            for half in range(2):
-                bank = spread(B1_ROW0 + (CHUNK // ROW) * c + 4 * half)
-                dst = b1_all[:].bitcast(F32)[:, half * N_PASS : (half + 1) * N_PASS]
-                if half == 0:
-                    nc.scalar.copy(out=dst, in_=bank[:])
-                else:
-                    nc.vector.tensor_copy(out=dst, in_=bank[:])
-            b1_tiles[c] = b1_all
 
         def first_layer(c):
             for j in range(CHUNK // N_PASS):
                 n = c * (CHUNK // N_PASS) + j
                 k, col = divmod(n * N_PASS, HIDDEN // PLANES)
-                h_ps = psum_mm.tile([P, N_PASS], F32, tag="mm", name="h_ps")
+                h_ps = psum.tile([P, N_PASS], F32, tag="bank", name="h_ps")
                 nc.tensor.matmul_mx(
                     out=h_ps[:],
                     lhsT=u_codes[:].bitcast(FP8X4),
@@ -172,26 +174,30 @@ def tile_mamba2backbone_pa_k_kernel(
                 nc.vector.tensor_tensor(
                     out=h[n // 2][:, (n % 2) * N_PASS : (n % 2 + 1) * N_PASS],
                     in0=h_ps[:],
-                    in1=b1_tiles[c][:, j * N_PASS : (j + 1) * N_PASS],
+                    in1=b1_all[:, n * N_PASS : (n + 1) * N_PASS],
                     op=ALU.add,
                 )
-            for i in range(c * (CHUNK // UNIT), (c + 1) * (CHUNK // UNIT)):
-                squares = work.tile([P, UNIT], BF16, name="squares")
-                nc.scalar.activation(out=squares[:], in_=h[i][:], func=FUNC.Square, accum_out=sums[:, i : i + 1])
+                if c == W1_CHUNKS - 1:
+                    squares = junk.tile([P, UNIT], BF16, name="squares")
+                    nc.scalar.activation(
+                        out=squares[:, 0:N_PASS],
+                        in_=h[n // 2][:, (n % 2) * N_PASS : (n % 2 + 1) * N_PASS],
+                        func=FUNC.Square,
+                        accum_out=sums[:, UNITS - 2 + j : UNITS - 1 + j],
+                    )
+            if c < W1_CHUNKS - 1:
+                for i in range(c * (CHUNK // UNIT), (c + 1) * (CHUNK // UNIT)):
+                    squares = junk.tile([P, UNIT], BF16, name="squares")
+                    nc.scalar.activation(out=squares[:], in_=h[i][:], func=FUNC.Square, accum_out=sums[:, i : i + 1])
 
-        for c in range(B1_LEAD):
-            spread_b1(c)
         for c in range(W1_CHUNKS):
-            if c + B1_LEAD < W1_CHUNKS:
-                spread_b1(c + B1_LEAD)
             first_layer(c)
 
         def scale_by_gain(i):
             nw_bank = spread(NW_ROW0 + (UNIT // ROW) * i)
             nc.vector.tensor_tensor(out=h[i][:], in0=h[i][:], in1=nw_bank[:].bitcast(BF16), op=ALU.mult)
 
-        for i in range(GAIN_LEAD):
-            scale_by_gain(i)
+        scale_by_gain(0)
 
         total = keep.tile([P, 1], F32)
         nc.vector.reduce_sum(out=total[:], in_=sums[:], axis=mybir.AxisListType.X)
@@ -201,6 +207,8 @@ def tile_mamba2backbone_pa_k_kernel(
         )
         rstd = keep.tile([P, 1], F32)
         nc.gpsimd.tensor_tensor(out=rstd[:], in0=mean_eps[:], in1=neg_half[:], op=ALU.pow)
+        for i in range(1, GAIN_LEAD):
+            scale_by_gain(i)
 
         acc = [psum_acc.tile([P, N_PASS], F32, name="acc%d" % half) for half in range(2)]
         g_rows_tiles = {}
@@ -220,7 +228,7 @@ def tile_mamba2backbone_pa_k_kernel(
 
         def turn(i):
             g_words = g_rows_tiles[i][:].bitcast(F32)
-            g_ps = psum_mm.tile([P, PASSES, 2, P], F32, tag="mm", name="g_ps")
+            g_ps = psum.tile([P, PASSES, 2, P], F32, tag="bank", name="g_ps")
             for s in range(PASSES):
                 for w in range(2):
                     first = w * (UNIT // PACK) + s * P

@@ -86,12 +86,15 @@ def tile_mamba2backbone_pa_k_kernel(
                 in_=tok_w1_scales[0, 4 * quad : 4 * quad + 4, :].bitcast(I32).rearrange("r (k c) -> k r c", k=PLANES),
             )
 
-        def load_w2_planes(a):
-            for quad in range(4):
-                nc.sync.dma_start(
-                    out=w2_planes[32 * quad : 32 * quad + 16, a, :].bitcast(I32),
-                    in_=tok_w2_scales[PLANES * a : PLANES * (a + 1), 4 * quad : 4 * quad + 4, :].bitcast(I32),
-                )
+        def load_w2_planes():
+            by_plane = tok_w2_scales.rearrange("(a k) q n -> k q a n", k=PLANES)
+            for quad in (0, 2, 1, 3):
+                for k in range(PLANES):
+                    first = 32 * quad + 4 * k
+                    nc.sync.dma_start(
+                        out=w2_planes[first : first + 4, :, :].bitcast(I32),
+                        in_=by_plane[k, 4 * quad : 4 * quad + 4, :, :].bitcast(I32),
+                    )
 
         w1_words = tok_w1_words[0].rearrange("p n t -> p (n t)").bitcast(I32)
         w2_words = tok_w2_words.rearrange("g p n t -> p g (n t)").bitcast(I32)
@@ -102,9 +105,8 @@ def tile_mamba2backbone_pa_k_kernel(
             w1_tiles.append(w1_tile)
         w2_tiles = []
         for i in range(UNITS):
-            if i % 8 == 0:
-                for a in range(i // 2, i // 2 + 4):
-                    load_w2_planes(a)
+            if i == 0:
+                load_w2_planes()
             w2_tile = weights.tile([P, CHUNK], U32, tag="w", name="w2_tile", align_bytes=64)
             nc.sync.dma_start(
                 out=w2_tile[:].bitcast(I32).rearrange("p (g n) -> p g n", g=2), in_=w2_words[:, 2 * i : 2 * i + 2, :]

@@ -74,6 +74,9 @@ def tile_mamba2backbone_pa_k_kernel(
 
         neg_half = keep.tile([P, 1], F32)
         nc.vector.memset(neg_half[:], -0.5)
+        spare = keep.tile([P, 1], F32)
+        nc.gpsimd.memset(spare[:], 1.0)
+        nc.gpsimd.tensor_tensor(out=spare[:], in0=spare[:], in1=neg_half[:], op=ALU.pow)
 
         w1_planes = keep.tile([P, HIDDEN // PLANES], U8, align_bytes=64)
         w2_planes = keep.tile([P, HIDDEN // K_PASS // PLANES, DETER], U8, align_bytes=64)
@@ -201,11 +204,10 @@ def tile_mamba2backbone_pa_k_kernel(
 
         scale_by_gain(0)
 
-        total = keep.tile([P, 1], F32)
-        nc.vector.reduce_sum(out=total[:], in_=sums[:], axis=mybir.AxisListType.X)
+        shares = keep.tile([P, UNITS + 2], F32)
         mean_eps = keep.tile([P, 1], F32)
         nc.vector.tensor_scalar(
-            out=mean_eps[:], in0=total[:], scalar1=1.0 / HIDDEN, scalar2=EPS, op0=ALU.mult, op1=ALU.add
+            out=shares[:], in0=sums[:], scalar1=1.0 / HIDDEN, scalar2=EPS, op0=ALU.mult, op1=ALU.add, accum_out=mean_eps[:]
         )
         rstd = keep.tile([P, 1], F32)
         nc.gpsimd.tensor_tensor(out=rstd[:], in0=mean_eps[:], in1=neg_half[:], op=ALU.pow)

@@ -46,17 +46,37 @@ def tile_mamba2backbone_pa_k_kernel(
         psum = stack.enter_context(tc.psum_pool(name="psum", bufs=6))
         psum_acc = stack.enter_context(tc.psum_pool(name="psum_acc", bufs=1))
 
+        u_sb = keep.tile([P, K_PASS], BF16)
+        act_sb = keep.tile([P, K_PASS - STOCH], BF16)
+        nc.scalar.dma_start(out=u_sb[:, 0:STOCH], in_=stoch)
+        nc.scalar.dma_start(out=act_sb[:], in_=action)
+
+        w1_words = tok_w1_words[0].rearrange("p n t -> p (n t)").bitcast(I32)
+        w2_words = tok_w2_words.rearrange("g p n t -> p g (n t)").bitcast(I32)
+        w1_tiles = []
+
+        def load_w1(c):
+            w1_tile = weights.tile([P, CHUNK], U32, tag="w", name="w1_tile", align_bytes=64)
+            nc.sync.dma_start(out=w1_tile[:].bitcast(I32), in_=w1_words[:, c * CHUNK : (c + 1) * CHUNK])
+            w1_tiles.append(w1_tile)
+
+        load_w1(0)
+
+        w1_planes = keep.tile([P, HIDDEN // PLANES], U8, align_bytes=64)
+        w2_planes = keep.tile([P, HIDDEN // K_PASS // PLANES, DETER], U8, align_bytes=64)
+        nc.vector.memset(w1_planes[:].bitcast(I32), 0)
+        for quad in range(4):
+            nc.sync.dma_start(
+                out=w1_planes[32 * quad : 32 * quad + 16, :].bitcast(I32),
+                in_=tok_w1_scales[0, 4 * quad : 4 * quad + 4, :].bitcast(I32).rearrange("r (k c) -> k r c", k=PLANES),
+            )
+
         zero_words = keep.tile([P, N_PASS // 2], F32)
         nc.vector.memset(zero_words[:], 0.0)
         zeros = zero_words[:].bitcast(BF16)
         for n in range(WARM):
             idle_ps = psum.tile([P, N_PASS], F32, tag="bank", name="idle_ps")
             nc.tensor.matmul(idle_ps[:], lhsT=zeros[:, 0:P], rhs=zeros, start=True, stop=True)
-
-        u_sb = keep.tile([P, K_PASS], BF16)
-        act_sb = keep.tile([P, K_PASS - STOCH], BF16)
-        nc.scalar.dma_start(out=u_sb[:, 0:STOCH], in_=stoch)
-        nc.scalar.dma_start(out=act_sb[:], in_=action)
 
         table = keep.tile([P, 2 * P], F32)
         nc.vector.memset(table[:, P : 2 * P], 0.0)
@@ -78,42 +98,31 @@ def tile_mamba2backbone_pa_k_kernel(
         nc.gpsimd.memset(spare[:], 1.0)
         nc.gpsimd.tensor_tensor(out=spare[:], in0=spare[:], in1=neg_half[:], op=ALU.pow)
 
-        w1_planes = keep.tile([P, HIDDEN // PLANES], U8, align_bytes=64)
-        w2_planes = keep.tile([P, HIDDEN // K_PASS // PLANES, DETER], U8, align_bytes=64)
-        nc.vector.memset(w1_planes[:].bitcast(I32), 0)
         nc.vector.memset(w2_planes[:].rearrange("p a n -> p (a n)").bitcast(I32), 0)
 
-        for quad in range(4):
-            nc.sync.dma_start(
-                out=w1_planes[32 * quad : 32 * quad + 16, :].bitcast(I32),
-                in_=tok_w1_scales[0, 4 * quad : 4 * quad + 4, :].bitcast(I32).rearrange("r (k c) -> k r c", k=PLANES),
-            )
-
         def load_w2_planes():
-            by_plane = tok_w2_scales.rearrange("(a k) q n -> k q a n", k=PLANES)
-            for quad in (0, 2, 1, 3):
+            by_row = tok_w2_scales.rearrange("(a k) (quad r) n -> k r quad a n", k=PLANES, r=4)
+            for r in range(4):
                 for k in range(PLANES):
-                    first = 32 * quad + 4 * k
                     nc.sync.dma_start(
-                        out=w2_planes[first : first + 4, :, :].bitcast(I32),
-                        in_=by_plane[k, 4 * quad : 4 * quad + 4, :, :].bitcast(I32),
+                        out=w2_planes[4 * k + r : P : 32, :, :].bitcast(I32), in_=by_row[k, r, :, :, :].bitcast(I32)
                     )
 
-        w1_words = tok_w1_words[0].rearrange("p n t -> p (n t)").bitcast(I32)
-        w2_words = tok_w2_words.rearrange("g p n t -> p g (n t)").bitcast(I32)
-        w1_tiles = []
-        for c in range(W1_CHUNKS):
-            w1_tile = weights.tile([P, CHUNK], U32, tag="w", name="w1_tile", align_bytes=64)
-            nc.sync.dma_start(out=w1_tile[:].bitcast(I32), in_=w1_words[:, c * CHUNK : (c + 1) * CHUNK])
-            w1_tiles.append(w1_tile)
+        for c in range(1, W1_CHUNKS):
+            load_w1(c)
+        load_w2_planes()
         w2_tiles = []
         for i in range(UNITS):
-            if i == 0:
-                load_w2_planes()
             w2_tile = weights.tile([P, CHUNK], U32, tag="w", name="w2_tile", align_bytes=64)
-            nc.sync.dma_start(
-                out=w2_tile[:].bitcast(I32).rearrange("p (g n) -> p g n", g=2), in_=w2_words[:, 2 * i : 2 * i + 2, :]
-            )
+            if i < UNITS - 1:
+                nc.sync.dma_start(
+                    out=w2_tile[:].bitcast(I32).rearrange("p (g n) -> p g n", g=2), in_=w2_words[:, 2 * i : 2 * i + 2, :]
+                )
+            else:
+                for s in range(2):
+                    nc.sync.dma_start(
+                        out=w2_tile[:, s * DETER : (s + 1) * DETER].bitcast(I32), in_=w2_words[:, 2 * i + s, :]
+                    )
             w2_tiles.append(w2_tile)
 
         turned_ps = psum.tile([P, N_PASS], F32, tag="bank", name="turned_ps")
@@ -202,17 +211,16 @@ def tile_mamba2backbone_pa_k_kernel(
             nw_bank = spread(NW_ROW0 + (UNIT // ROW) * i)
             nc.vector.tensor_tensor(out=h[i][:], in0=h[i][:], in1=nw_bank[:].bitcast(BF16), op=ALU.mult)
 
-        scale_by_gain(0)
+        for i in range(GAIN_LEAD):
+            scale_by_gain(i)
 
         shares = keep.tile([P, UNITS + 2], F32)
         mean_eps = keep.tile([P, 1], F32)
-        nc.vector.tensor_scalar(
-            out=shares[:], in0=sums[:], scalar1=1.0 / HIDDEN, scalar2=EPS, op0=ALU.mult, op1=ALU.add, accum_out=mean_eps[:]
+        nc.scalar.activation(
+            out=shares[:], in_=sums[:], func=FUNC.Copy, scale=1.0 / HIDDEN, bias=EPS / (UNITS + 2), accum_out=mean_eps[:]
         )
         rstd = keep.tile([P, 1], F32)
         nc.gpsimd.tensor_tensor(out=rstd[:], in0=mean_eps[:], in1=neg_half[:], op=ALU.pow)
-        for i in range(1, GAIN_LEAD):
-            scale_by_gain(i)
 
         acc = [psum_acc.tile([P, N_PASS], F32, name="acc%d" % half) for half in range(2)]
         g_rows_tiles = {}
@@ -255,10 +263,10 @@ def tile_mamba2backbone_pa_k_kernel(
 
         def second_layer(i):
             g_codes, g_plane = g_tiles[i]
-            for s in range(PASSES):
+            for s, half in [(s, half) for s in range(PASSES) for half in range(2)]:
                 g_pass = i * PASSES + s
                 a, k = divmod(g_pass, PLANES)
-                for half in range(2):
+                if True:
                     nc.tensor.matmul_mx(
                         out=acc[half][:],
                         lhsT=g_codes[:, s * P : (s + 1) * P].bitcast(FP8X4),
@@ -269,18 +277,27 @@ def tile_mamba2backbone_pa_k_kernel(
                         stop=(g_pass == HIDDEN // K_PASS - 1),
                     )
 
-        for j in range(UNITS + 3):
-            if j + GAIN_LEAD < UNITS:
-                scale_by_gain(j + GAIN_LEAD)
-            if j < UNITS:
-                activate(j)
-            if 1 <= j <= UNITS:
-                turn(j - 1)
-                group(j - 1)
-            if 2 <= j <= UNITS + 1:
-                quantise(j - 2)
-            if j >= 3:
-                second_layer(j - 3)
+        groups = [[0], [1]] + [[i, i + 1] for i in range(2, UNITS, 2)]
+        gained = GAIN_LEAD
+        for t in range(len(groups) + 2):
+            now = groups[t] if t < len(groups) else []
+            before = groups[t - 1] if 1 <= t <= len(groups) else []
+            ready = groups[t - 2] if t >= 2 else []
+            for i in before:
+                turn(i)
+            if now:
+                for i in range(gained, min(UNITS, now[-1] + GAIN_LEAD + 1)):
+                    scale_by_gain(i)
+                gained = max(gained, min(UNITS, now[-1] + GAIN_LEAD + 1))
+            for n in range(max(len(now), len(before))):
+                if n < len(now):
+                    activate(now[n])
+                if n < len(before):
+                    group(before[n])
+            for i in before:
+                quantise(i)
+            for i in ready:
+                second_layer(i)
 
         out_sb = keep.tile([P, DETER], F32)
         for half in range(2):

@@ -51,6 +51,13 @@ def tile_mamba2backbone_pa_k_kernel(
         nc.scalar.dma_start(out=u_sb[:, 0:STOCH], in_=stoch)
         nc.scalar.dma_start(out=act_sb[:], in_=action)
 
+        table = keep.tile([P, 2 * P], F32)
+        nc.vector.memset(table[:, P : 2 * P], 0.0)
+        nc.scalar.dma_start(out=table[0:64, 0:P], in_=tok_b1.bitcast(F32).rearrange("(r w) -> r w", w=P))
+        nc.scalar.dma_start(out=table[64:P, 0:P], in_=tok_nw.bitcast(F32).rearrange("(r w) -> r w", w=P))
+        nc.scalar.dma_start(out=table[0:4, P : 2 * P], in_=tok_b2.bitcast(F32).rearrange("(r w) -> r w", w=P))
+        B1_ROW0, NW_ROW0, B2_ROW0 = 0, 64, P
+
         w1_words = tok_w1_words[0].rearrange("p n t -> p (n t)").bitcast(I32)
         w2_words = tok_w2_words.rearrange("g p n t -> p g (n t)").bitcast(I32)
         w1_tiles = []
@@ -62,14 +69,9 @@ def tile_mamba2backbone_pa_k_kernel(
 
         load_w1(0)
 
-        w1_planes = keep.tile([P, HIDDEN // PLANES], U8, align_bytes=64)
-        w2_planes = keep.tile([P, HIDDEN // K_PASS // PLANES, DETER], U8, align_bytes=64)
-        nc.vector.memset(w1_planes[:].bitcast(I32), 0)
-        for quad in range(4):
-            nc.sync.dma_start(
-                out=w1_planes[32 * quad : 32 * quad + 16, :].bitcast(I32),
-                in_=tok_w1_scales[0, 4 * quad : 4 * quad + 4, :].bitcast(I32).rearrange("r (k c) -> k r c", k=PLANES),
-            )
+        warm = keep.tile([P, 1], F32)
+        nc.vector.memset(warm[:], 0.0)
+        nc.scalar.activation(out=warm[:], in_=warm[:], func=FUNC.Silu)
 
         zero_words = keep.tile([P, N_PASS // 2], F32)
         nc.vector.memset(zero_words[:], 0.0)
@@ -78,25 +80,23 @@ def tile_mamba2backbone_pa_k_kernel(
             idle_ps = psum.tile([P, N_PASS], F32, tag="bank", name="idle_ps")
             nc.tensor.matmul(idle_ps[:], lhsT=zeros[:, 0:P], rhs=zeros, start=True, stop=True)
 
-        table = keep.tile([P, 2 * P], F32)
-        nc.vector.memset(table[:, P : 2 * P], 0.0)
-        nc.scalar.dma_start(out=table[0:64, 0:P], in_=tok_b1.bitcast(F32).rearrange("(r w) -> r w", w=P))
-        nc.scalar.dma_start(out=table[64:P, 0:P], in_=tok_nw.bitcast(F32).rearrange("(r w) -> r w", w=P))
-        nc.scalar.dma_start(out=table[0:4, P : 2 * P], in_=tok_b2.bitcast(F32).rearrange("(r w) -> r w", w=P))
-        B1_ROW0, NW_ROW0, B2_ROW0 = 0, 64, P
-
         ident = keep.tile([P, P], F32)
         make_identity(nc, ident[:])
-
-        warm = keep.tile([P, 1], F32)
-        nc.vector.memset(warm[:], 0.0)
-        nc.scalar.activation(out=warm[:], in_=warm[:], func=FUNC.Silu)
 
         neg_half = keep.tile([P, 1], F32)
         nc.vector.memset(neg_half[:], -0.5)
         spare = keep.tile([P, 1], F32)
         nc.gpsimd.memset(spare[:], 1.0)
         nc.gpsimd.tensor_tensor(out=spare[:], in0=spare[:], in1=neg_half[:], op=ALU.pow)
+
+        w1_planes = keep.tile([P, HIDDEN // PLANES], U8, align_bytes=64)
+        w2_planes = keep.tile([P, HIDDEN // K_PASS // PLANES, DETER], U8, align_bytes=64)
+        nc.vector.memset(w1_planes[:].bitcast(I32), 0)
+        for quad in range(4):
+            nc.sync.dma_start(
+                out=w1_planes[32 * quad : 32 * quad + 16, :].bitcast(I32),
+                in_=tok_w1_scales[0, 4 * quad : 4 * quad + 4, :].bitcast(I32).rearrange("r (k c) -> k r c", k=PLANES),
+            )
 
         nc.vector.memset(w2_planes[:].rearrange("p a n -> p (a n)").bitcast(I32), 0)
 

@@ -28,7 +28,7 @@ W1_CHUNKS = HIDDEN // CHUNK
 ROW = 256
 PLANES = 4
 WARM = 6
-GAIN_LEAD = 2
+GAIN_LEAD = 3
 
 FLOPS = 2 * P * K_PASS * HIDDEN + 2 * P * HIDDEN * DETER
 
@@ -119,9 +119,11 @@ def tile_mamba2backbone_pa_k_kernel(
                     out=w2_tile[:].bitcast(I32).rearrange("p (g n) -> p g n", g=2), in_=w2_words[:, 2 * i : 2 * i + 2, :]
                 )
             else:
-                for s in range(2):
+                nc.sync.dma_start(out=w2_tile[:, 0:DETER].bitcast(I32), in_=w2_words[:, 2 * i, :])
+                for half in range(2):
                     nc.sync.dma_start(
-                        out=w2_tile[:, s * DETER : (s + 1) * DETER].bitcast(I32), in_=w2_words[:, 2 * i + s, :]
+                        out=w2_tile[:, DETER + half * N_PASS : DETER + (half + 1) * N_PASS].bitcast(I32),
+                        in_=w2_words[:, 2 * i + 1, half * N_PASS : (half + 1) * N_PASS],
                     )
             w2_tiles.append(w2_tile)
 
@@ -263,7 +265,10 @@ def tile_mamba2backbone_pa_k_kernel(
 
         def second_layer(i):
             g_codes, g_plane = g_tiles[i]
-            for s, half in [(s, half) for s in range(PASSES) for half in range(2)]:
+            steps = [(s, half) for s in range(PASSES) for half in range(2)]
+            if i == UNITS - 1:
+                steps = [(s, half) for half in range(2) for s in range(PASSES)]
+            for s, half in steps:
                 g_pass = i * PASSES + s
                 a, k = divmod(g_pass, PLANES)
                 if True:

@@ -40,7 +40,7 @@ def tile_mamba2backbone_pa_k_kernel(
     with ExitStack() as stack:
         stack.enter_context(tc.manual_schedule())
         keep = stack.enter_context(tc.tile_pool(name="keep", bufs=1))
-        weights = stack.enter_context(tc.tile_pool(name="weights", bufs=10))
+        weights = stack.enter_context(tc.tile_pool(name="weights", bufs=5))
         work = stack.enter_context(tc.tile_pool(name="work", bufs=4))
         junk = stack.enter_context(tc.tile_pool(name="junk", bufs=2))
         psum = stack.enter_context(tc.psum_pool(name="psum", bufs=6))
@@ -61,13 +61,11 @@ def tile_mamba2backbone_pa_k_kernel(
         w1_words = tok_w1_words[0].rearrange("p n t -> p (n t)").bitcast(I32)
         w2_words = tok_w2_words.rearrange("g p n t -> p g (n t)").bitcast(I32)
         w1_tiles = []
-
-        def load_w1(c):
-            w1_tile = weights.tile([P, CHUNK], U32, tag="w", name="w1_tile", align_bytes=64)
-            nc.sync.dma_start(out=w1_tile[:].bitcast(I32), in_=w1_words[:, c * CHUNK : (c + 1) * CHUNK])
+        for t in range(W1_CHUNKS // 2):
+            w1_tile = weights.tile([P, 2 * CHUNK], U32, tag="w", name="w1_tile", align_bytes=64)
             w1_tiles.append(w1_tile)
 
-        load_w1(0)
+        nc.sync.dma_start(out=w1_tiles[0][:, 0:CHUNK].bitcast(I32), in_=w1_words[:, 0:CHUNK])
 
         warm = keep.tile([P, 1], F32)
         nc.vector.memset(warm[:], 0.0)
@@ -108,28 +106,37 @@ def tile_mamba2backbone_pa_k_kernel(
                         out=w2_planes[4 * k + r : P : 32, :, :].bitcast(I32), in_=by_row[k, r, :, :, :].bitcast(I32)
                     )
 
-        for c in range(1, W1_CHUNKS):
-            load_w1(c)
+        nc.sync.dma_start(out=w1_tiles[0][:, CHUNK : 2 * CHUNK].bitcast(I32), in_=w1_words[:, CHUNK : 2 * CHUNK])
+        for t in range(1, W1_CHUNKS // 2):
+            nc.sync.dma_start(out=w1_tiles[t][:].bitcast(I32), in_=w1_words[:, 2 * t * CHUNK : 2 * (t + 1) * CHUNK])
         load_w2_planes()
         w2_tiles = []
-        for i in range(UNITS):
-            w2_tile = weights.tile([P, CHUNK], U32, tag="w", name="w2_tile", align_bytes=64)
-            if i < UNITS - 1:
+        for t in range(UNITS // 2):
+            w2_tile = weights.tile([P, 2 * CHUNK], U32, tag="w", name="w2_tile", align_bytes=64)
+            if t < UNITS // 2 - 1:
                 nc.sync.dma_start(
-                    out=w2_tile[:].bitcast(I32).rearrange("p (g n) -> p g n", g=2), in_=w2_words[:, 2 * i : 2 * i + 2, :]
+                    out=w2_tile[:].bitcast(I32).rearrange("p (g n) -> p g n", g=4), in_=w2_words[:, 4 * t : 4 * t + 4, :]
                 )
             else:
-                nc.sync.dma_start(out=w2_tile[:, 0:DETER].bitcast(I32), in_=w2_words[:, 2 * i, :])
+                nc.sync.dma_start(
+                    out=w2_tile[:, 0:CHUNK].bitcast(I32).rearrange("p (g n) -> p g n", g=2),
+                    in_=w2_words[:, 4 * t : 4 * t + 2, :],
+                )
+                nc.sync.dma_start(out=w2_tile[:, CHUNK : CHUNK + DETER].bitcast(I32), in_=w2_words[:, 4 * t + 2, :])
                 for half in range(2):
+                    first = CHUNK + DETER + half * N_PASS
                     nc.sync.dma_start(
-                        out=w2_tile[:, DETER + half * N_PASS : DETER + (half + 1) * N_PASS].bitcast(I32),
-                        in_=w2_words[:, 2 * i + 1, half * N_PASS : (half + 1) * N_PASS],
+                        out=w2_tile[:, first : first + N_PASS].bitcast(I32),
+                        in_=w2_words[:, 4 * t + 3, half * N_PASS : (half + 1) * N_PASS],
                     )
             w2_tiles.append(w2_tile)
 
         turned_ps = psum.tile([P, N_PASS], F32, tag="bank", name="turned_ps")
         for half in range(2):
             nc.tensor.transpose(turned_ps[:, half * P : (half + 1) * P], table[:, half * P : (half + 1) * P], ident[:])
+        nc.vector.tensor_scalar(
+            out=u_sb[:, STOCH:K_PASS], in0=act_sb[:], scalar1=-1.0, scalar2=1.0, op0=ALU.max, op1=ALU.min
+        )
         turned = keep.tile([P, 2 * P], F32)
         nc.vector.tensor_copy(out=turned[:], in_=turned_ps[:, 0 : 2 * P])
 
@@ -143,26 +150,28 @@ def tile_mamba2backbone_pa_k_kernel(
                 )
             return bank
 
-        nc.vector.tensor_scalar(
-            out=u_sb[:, STOCH:K_PASS], in0=act_sb[:], scalar1=-1.0, scalar2=1.0, op0=ALU.max, op1=ALU.min
-        )
-        u_words = u_sb[:].bitcast(F32)
-        u_ps = psum.tile([P, 2, P], F32, tag="bank", name="u_ps")
-        for w in range(2):
-            nc.tensor.transpose(u_ps[:, w, :], u_words[:, w : K_PASS // 2 : 2], ident[:])
-        u_grouped = keep.tile([P, P * PACK], BF16, align_bytes=64)
-        nc.vector.tensor_copy(
-            out=u_grouped[:].bitcast(F32).rearrange("p (b w) -> p b w", w=2), in_=u_ps[:].rearrange("p w b -> p b w")
-        )
-        u_codes = keep.tile([P, P], U32, align_bytes=64)
-        u_plane = keep.tile([P, P], U8, align_bytes=64)
-        nc.vector.quantize_mx(out=u_codes[:].bitcast(FP8X4), scales=u_plane[:], in_=u_grouped[:])
-
         h = [keep.tile([P, UNIT], F32, name="h%d" % i) for i in range(UNITS)]
         sums = keep.tile([P, UNITS + 2], F32)
 
+        u_codes = keep.tile([P, P], U32, align_bytes=64)
+        u_plane = keep.tile([P, P], U8, align_bytes=64)
+
+        def quantise_u():
+            u_words = u_sb[:].bitcast(F32)
+            u_ps = psum.tile([P, 2, P], F32, tag="bank", name="u_ps")
+            for w in range(2):
+                nc.tensor.transpose(u_ps[:, w, :], u_words[:, w : K_PASS // 2 : 2], ident[:])
+            u_grouped = keep.tile([P, P * PACK], BF16, align_bytes=64)
+            nc.vector.tensor_copy(
+                out=u_grouped[:].bitcast(F32).rearrange("p (b w) -> p b w", w=2), in_=u_ps[:].rearrange("p w b -> p b w")
+            )
+            nc.vector.quantize_mx(out=u_codes[:].bitcast(FP8X4), scales=u_plane[:], in_=u_grouped[:])
+
+
         b1_all = keep.tile([P, HIDDEN], BF16)
         for i in range(UNITS):
+            if i == UNITS // 2:
+                quantise_u()
             bank = spread(B1_ROW0 + (UNIT // ROW) * i)
             dst = b1_all[:, i * UNIT : (i + 1) * UNIT].bitcast(F32)
             if i % 2 == 0:
@@ -182,7 +191,7 @@ def tile_mamba2backbone_pa_k_kernel(
                     out=h_ps[:],
                     lhsT=u_codes[:].bitcast(FP8X4),
                     lhsT_scale=u_plane[:],
-                    rhs=w1_tiles[c][:, j * N_PASS : (j + 1) * N_PASS].bitcast(FP8X4),
+                    rhs=w1_tiles[c // 2][:, (c % 2) * CHUNK + j * N_PASS : (c % 2) * CHUNK + (j + 1) * N_PASS].bitcast(FP8X4),
                     rhs_scale=w1_planes[4 * k : P, col : col + N_PASS],
                     start=True,
                     stop=True,
@@ -263,6 +272,9 @@ def tile_mamba2backbone_pa_k_kernel(
             nc.vector.quantize_mx(out=g_codes[:].bitcast(FP8X4), scales=g_plane[:], in_=g_tiles[i][:])
             g_tiles[i] = (g_codes, g_plane)
 
+        def w2_col(i, s, half):
+            return (i % 2) * CHUNK + s * DETER + half * N_PASS
+
         def second_layer(i):
             g_codes, g_plane = g_tiles[i]
             steps = [(s, half) for s in range(PASSES) for half in range(2)]
@@ -276,7 +288,7 @@ def tile_mamba2backbone_pa_k_kernel(
                         out=acc[half][:],
                         lhsT=g_codes[:, s * P : (s + 1) * P].bitcast(FP8X4),
                         lhsT_scale=g_plane[:, s * P : (s + 1) * P],
-                        rhs=w2_tiles[i][:, s * DETER + half * N_PASS : s * DETER + (half + 1) * N_PASS].bitcast(FP8X4),
+                        rhs=w2_tiles[i // 2][:, w2_col(i, s, half) : w2_col(i, s, half) + N_PASS].bitcast(FP8X4),
                         rhs_scale=w2_planes[4 * k : P, a, half * N_PASS : (half + 1) * N_PASS],
                         start=(g_pass == 0),
                         stop=(g_pass == HIDDEN // K_PASS - 1),

from contextlib import ExitStack

import concourse.mybir as mybir
from concourse.masks import make_identity

F32 = mybir.dt.float32
BF16 = mybir.dt.bfloat16
I32 = mybir.dt.int32
U32 = mybir.dt.uint32
U8 = mybir.dt.uint8
FP8X4 = mybir.dt.float8_e4m3fn_x4
ALU = mybir.AluOpType
FUNC = mybir.ActivationFunctionType

P = 128
PACK = 4
K_PASS = P * PACK
N_PASS = 512
STOCH = 256
HIDDEN = 16384
DETER = 1024
EPS = 1e-4

CHUNK = 2048
UNIT = 1024
UNITS = HIDDEN // UNIT
W1_CHUNKS = HIDDEN // CHUNK
ROW = 256
PLANES = 4
WARM = 6
GAIN_LEAD = 3

FLOPS = 2 * P * K_PASS * HIDDEN + 2 * P * HIDDEN * DETER


def tile_mamba2backbone_pa_k_kernel(
    tc, stoch, action, tok_w1_words, tok_w1_scales, tok_b1, tok_nw, tok_w2_words, tok_w2_scales, tok_b2, out
):
    nc = tc.nc
    with ExitStack() as stack:
        stack.enter_context(tc.manual_schedule())
        keep = stack.enter_context(tc.tile_pool(name="keep", bufs=1))
        weights = stack.enter_context(tc.tile_pool(name="weights", bufs=5))
        work = stack.enter_context(tc.tile_pool(name="work", bufs=4))
        junk = stack.enter_context(tc.tile_pool(name="junk", bufs=2))
        psum = stack.enter_context(tc.psum_pool(name="psum", bufs=6))
        psum_acc = stack.enter_context(tc.psum_pool(name="psum_acc", bufs=1))

        u_sb = keep.tile([P, K_PASS], BF16)
        act_sb = keep.tile([P, K_PASS - STOCH], BF16)
        nc.scalar.dma_start(out=u_sb[:, 0:STOCH], in_=stoch)
        nc.scalar.dma_start(out=act_sb[:], in_=action)

        table = keep.tile([P, 2 * P], F32)
        nc.vector.memset(table[:, P : 2 * P], 0.0)
        nc.scalar.dma_start(out=table[0:64, 0:P], in_=tok_b1.bitcast(F32).rearrange("(r w) -> r w", w=P))
        nc.scalar.dma_start(out=table[64:P, 0:P], in_=tok_nw.bitcast(F32).rearrange("(r w) -> r w", w=P))
        nc.scalar.dma_start(out=table[0:4, P : 2 * P], in_=tok_b2.bitcast(F32).rearrange("(r w) -> r w", w=P))
        B1_ROW0, NW_ROW0, B2_ROW0 = 0, 64, P

        w1_words = tok_w1_words[0].rearrange("p n t -> p (n t)").bitcast(I32)
        w2_words = tok_w2_words.rearrange("g p n t -> p g (n t)").bitcast(I32)
        w1_tiles = []
        for t in range(W1_CHUNKS // 2):
            w1_tile = weights.tile([P, 2 * CHUNK], U32, tag="w", name="w1_tile", align_bytes=64)
            w1_tiles.append(w1_tile)

        nc.sync.dma_start(out=w1_tiles[0][:, 0:CHUNK].bitcast(I32), in_=w1_words[:, 0:CHUNK])

        warm = keep.tile([P, 1], F32)
        nc.vector.memset(warm[:], 0.0)
        nc.scalar.activation(out=warm[:], in_=warm[:], func=FUNC.Silu)

        zero_words = keep.tile([P, N_PASS // 2], F32)
        nc.vector.memset(zero_words[:], 0.0)
        zeros = zero_words[:].bitcast(BF16)
        for n in range(WARM):
            idle_ps = psum.tile([P, N_PASS], F32, tag="bank", name="idle_ps")
            nc.tensor.matmul(idle_ps[:], lhsT=zeros[:, 0:P], rhs=zeros, start=True, stop=True)

        ident = keep.tile([P, P], F32)
        make_identity(nc, ident[:])

        neg_half = keep.tile([P, 1], F32)
        nc.vector.memset(neg_half[:], -0.5)
        spare = keep.tile([P, 1], F32)
        nc.gpsimd.memset(spare[:], 1.0)
        nc.gpsimd.tensor_tensor(out=spare[:], in0=spare[:], in1=neg_half[:], op=ALU.pow)

        w1_planes = keep.tile([P, HIDDEN // PLANES], U8, align_bytes=64)
        w2_planes = keep.tile([P, HIDDEN // K_PASS // PLANES, DETER], U8, align_bytes=64)
        nc.vector.memset(w1_planes[:].bitcast(I32), 0)
        for quad in range(4):
            nc.sync.dma_start(
                out=w1_planes[32 * quad : 32 * quad + 16, :].bitcast(I32),
                in_=tok_w1_scales[0, 4 * quad : 4 * quad + 4, :].bitcast(I32).rearrange("r (k c) -> k r c", k=PLANES),
            )

        nc.vector.memset(w2_planes[:].rearrange("p a n -> p (a n)").bitcast(I32), 0)

        def load_w2_planes():
            by_row = tok_w2_scales.rearrange("(a k) (quad r) n -> k r quad a n", k=PLANES, r=4)
            for r in range(4):
                for k in range(PLANES):
                    nc.sync.dma_start(
                        out=w2_planes[4 * k + r : P : 32, :, :].bitcast(I32), in_=by_row[k, r, :, :, :].bitcast(I32)
                    )

        nc.sync.dma_start(out=w1_tiles[0][:, CHUNK : 2 * CHUNK].bitcast(I32), in_=w1_words[:, CHUNK : 2 * CHUNK])
        for t in range(1, W1_CHUNKS // 2):
            nc.sync.dma_start(out=w1_tiles[t][:].bitcast(I32), in_=w1_words[:, 2 * t * CHUNK : 2 * (t + 1) * CHUNK])
        load_w2_planes()
        w2_tiles = []
        for t in range(UNITS // 2):
            w2_tile = weights.tile([P, 2 * CHUNK], U32, tag="w", name="w2_tile", align_bytes=64)
            if t < UNITS // 2 - 1:
                nc.sync.dma_start(
                    out=w2_tile[:].bitcast(I32).rearrange("p (g n) -> p g n", g=4), in_=w2_words[:, 4 * t : 4 * t + 4, :]
                )
            else:
                nc.sync.dma_start(
                    out=w2_tile[:, 0:CHUNK].bitcast(I32).rearrange("p (g n) -> p g n", g=2),
                    in_=w2_words[:, 4 * t : 4 * t + 2, :],
                )
                nc.sync.dma_start(out=w2_tile[:, CHUNK : CHUNK + DETER].bitcast(I32), in_=w2_words[:, 4 * t + 2, :])
                for half in range(2):
                    first = CHUNK + DETER + half * N_PASS
                    nc.sync.dma_start(
                        out=w2_tile[:, first : first + N_PASS].bitcast(I32),
                        in_=w2_words[:, 4 * t + 3, half * N_PASS : (half + 1) * N_PASS],
                    )
            w2_tiles.append(w2_tile)

        turned_ps = psum.tile([P, N_PASS], F32, tag="bank", name="turned_ps")
        for half in range(2):
            nc.tensor.transpose(turned_ps[:, half * P : (half + 1) * P], table[:, half * P : (half + 1) * P], ident[:])
        nc.vector.tensor_scalar(
            out=u_sb[:, STOCH:K_PASS], in0=act_sb[:], scalar1=-1.0, scalar2=1.0, op0=ALU.max, op1=ALU.min
        )
        turned = keep.tile([P, 2 * P], F32)
        nc.vector.tensor_copy(out=turned[:], in_=turned_ps[:, 0 : 2 * P])

        def spread(first_row):
            bank = psum.tile([P, N_PASS], F32, tag="bank", name="bank")
            for r in range(4):
                nc.tensor.transpose(
                    bank[:, r * P : (r + 1) * P],
                    turned[:, first_row + r : first_row + r + 1].to_broadcast([P, P]),
                    ident[:],
                )
            return bank

        h = [keep.tile([P, UNIT], F32, name="h%d" % i) for i in range(UNITS)]
        sums = keep.tile([P, UNITS + 2], F32)

        u_codes = keep.tile([P, P], U32, align_bytes=64)
        u_plane = keep.tile([P, P], U8, align_bytes=64)

        def quantise_u():
            u_words = u_sb[:].bitcast(F32)
            u_ps = psum.tile([P, 2, P], F32, tag="bank", name="u_ps")
            for w in range(2):
                nc.tensor.transpose(u_ps[:, w, :], u_words[:, w : K_PASS // 2 : 2], ident[:])
            u_grouped = keep.tile([P, P * PACK], BF16, align_bytes=64)
            nc.vector.tensor_copy(
                out=u_grouped[:].bitcast(F32).rearrange("p (b w) -> p b w", w=2), in_=u_ps[:].rearrange("p w b -> p b w")
            )
            nc.vector.quantize_mx(out=u_codes[:].bitcast(FP8X4), scales=u_plane[:], in_=u_grouped[:])


        b1_all = keep.tile([P, HIDDEN], BF16)
        for i in range(UNITS):
            if i == UNITS // 2:
                quantise_u()
            bank = spread(B1_ROW0 + (UNIT // ROW) * i)
            dst = b1_all[:, i * UNIT : (i + 1) * UNIT].bitcast(F32)
            if i % 2 == 0:
                nc.scalar.copy(out=dst, in_=bank[:])
            else:
                nc.vector.tensor_copy(out=dst, in_=bank[:])
        b2_bank = spread(B2_ROW0)
        b2_all = keep.tile([P, DETER], BF16)
        nc.scalar.copy(out=b2_all[:].bitcast(F32), in_=b2_bank[:])

        def first_layer(c):
            for j in range(CHUNK // N_PASS):
                n = c * (CHUNK // N_PASS) + j
                k, col = divmod(n * N_PASS, HIDDEN // PLANES)
                h_ps = psum.tile([P, N_PASS], F32, tag="bank", name="h_ps")
                nc.tensor.matmul_mx(
                    out=h_ps[:],
                    lhsT=u_codes[:].bitcast(FP8X4),
                    lhsT_scale=u_plane[:],
                    rhs=w1_tiles[c // 2][:, (c % 2) * CHUNK + j * N_PASS : (c % 2) * CHUNK + (j + 1) * N_PASS].bitcast(FP8X4),
                    rhs_scale=w1_planes[4 * k : P, col : col + N_PASS],
                    start=True,
                    stop=True,
                )
                nc.vector.tensor_tensor(
                    out=h[n // 2][:, (n % 2) * N_PASS : (n % 2 + 1) * N_PASS],
                    in0=h_ps[:],
                    in1=b1_all[:, n * N_PASS : (n + 1) * N_PASS],
                    op=ALU.add,
                )
                if c == W1_CHUNKS - 1:
                    squares = junk.tile([P, UNIT], BF16, name="squares")
                    nc.scalar.activation(
                        out=squares[:, 0:N_PASS],
                        in_=h[n // 2][:, (n % 2) * N_PASS : (n % 2 + 1) * N_PASS],
                        func=FUNC.Square,
                        accum_out=sums[:, UNITS - 2 + j : UNITS - 1 + j],
                    )
            if c < W1_CHUNKS - 1:
                for i in range(c * (CHUNK // UNIT), (c + 1) * (CHUNK // UNIT)):
                    squares = junk.tile([P, UNIT], BF16, name="squares")
                    nc.scalar.activation(out=squares[:], in_=h[i][:], func=FUNC.Square, accum_out=sums[:, i : i + 1])

        for c in range(W1_CHUNKS):
            first_layer(c)

        def scale_by_gain(i):
            nw_bank = spread(NW_ROW0 + (UNIT // ROW) * i)
            nc.vector.tensor_tensor(out=h[i][:], in0=h[i][:], in1=nw_bank[:].bitcast(BF16), op=ALU.mult)

        for i in range(GAIN_LEAD):
            scale_by_gain(i)

        shares = keep.tile([P, UNITS + 2], F32)
        mean_eps = keep.tile([P, 1], F32)
        nc.scalar.activation(
            out=shares[:], in_=sums[:], func=FUNC.Copy, scale=1.0 / HIDDEN, bias=EPS / (UNITS + 2), accum_out=mean_eps[:]
        )
        rstd = keep.tile([P, 1], F32)
        nc.gpsimd.tensor_tensor(out=rstd[:], in0=mean_eps[:], in1=neg_half[:], op=ALU.pow)

        acc = [psum_acc.tile([P, N_PASS], F32, name="acc%d" % half) for half in range(2)]
        g_rows_tiles = {}
        g_ps_tiles = {}
        g_tiles = {}
        PASSES = UNIT // K_PASS

        def activate(i):
            g_rows = work.tile([P, UNIT], BF16, name="g_rows")
            nc.scalar.activation(
                out=g_rows[:].rearrange("b (w q e) -> b w q e", w=2, e=2),
                in_=h[i][:].rearrange("b (q w e) -> b w q e", w=2, e=2),
                func=FUNC.Silu,
                scale=rstd[:, 0:1],
            )
            g_rows_tiles[i] = g_rows

        def turn(i):
            g_words = g_rows_tiles[i][:].bitcast(F32)
            g_ps = psum.tile([P, PASSES, 2, P], F32, tag="bank", name="g_ps")
            for s in range(PASSES):
                for w in range(2):
                    first = w * (UNIT // PACK) + s * P
                    nc.tensor.transpose(g_ps[:, s, w, :], g_words[:, first : first + P], ident[:])
            g_ps_tiles[i] = g_ps

        def group(i):
            grouped = work.tile([P, UNIT], BF16, name="grouped", align_bytes=64)
            nc.scalar.copy(
                out=grouped[:].bitcast(F32).rearrange("p (s b w) -> p s b w", s=PASSES, w=2),
                in_=g_ps_tiles[i][:].rearrange("p s w b -> p s b w"),
            )
            g_tiles[i] = grouped

        def quantise(i):
            g_codes = work.tile([P, UNIT // PACK], U32, name="g_codes", align_bytes=64)
            g_plane = work.tile([P, UNIT // PACK], U8, name="g_plane", align_bytes=64)
            nc.vector.quantize_mx(out=g_codes[:].bitcast(FP8X4), scales=g_plane[:], in_=g_tiles[i][:])
            g_tiles[i] = (g_codes, g_plane)

        def w2_col(i, s, half):
            return (i % 2) * CHUNK + s * DETER + half * N_PASS

        def second_layer(i):
            g_codes, g_plane = g_tiles[i]
            steps = [(s, half) for s in range(PASSES) for half in range(2)]
            if i == UNITS - 1:
                steps = [(s, half) for half in range(2) for s in range(PASSES)]
            for s, half in steps:
                g_pass = i * PASSES + s
                a, k = divmod(g_pass, PLANES)
                if True:
                    nc.tensor.matmul_mx(
                        out=acc[half][:],
                        lhsT=g_codes[:, s * P : (s + 1) * P].bitcast(FP8X4),
                        lhsT_scale=g_plane[:, s * P : (s + 1) * P],
                        rhs=w2_tiles[i // 2][:, w2_col(i, s, half) : w2_col(i, s, half) + N_PASS].bitcast(FP8X4),
                        rhs_scale=w2_planes[4 * k : P, a, half * N_PASS : (half + 1) * N_PASS],
                        start=(g_pass == 0),
                        stop=(g_pass == HIDDEN // K_PASS - 1),
                    )

        groups = [[0], [1]] + [[i, i + 1] for i in range(2, UNITS, 2)]
        gained = GAIN_LEAD
        for t in range(len(groups) + 2):
            now = groups[t] if t < len(groups) else []
            before = groups[t - 1] if 1 <= t <= len(groups) else []
            ready = groups[t - 2] if t >= 2 else []
            for i in before:
                turn(i)
            if now:
                for i in range(gained, min(UNITS, now[-1] + GAIN_LEAD + 1)):
                    scale_by_gain(i)
                gained = max(gained, min(UNITS, now[-1] + GAIN_LEAD + 1))
            for n in range(max(len(now), len(before))):
                if n < len(now):
                    activate(now[n])
                if n < len(before):
                    group(before[n])
            for i in before:
                quantise(i)
            for i in ready:
                second_layer(i)

        out_sb = keep.tile([P, DETER], F32)
        for half in range(2):
            cols = slice(half * N_PASS, (half + 1) * N_PASS)
            nc.vector.tensor_tensor(out=out_sb[:, cols], in0=acc[half][:], in1=b2_all[:, cols], op=ALU.add)
            nc.sync.dma_start(out=out[:, cols], in_=out_sb[:, cols])
